import numpy as np
import ml_dtypes

BF16 = ml_dtypes.bfloat16


def bf(x):
    return np.asarray(x, np.float32).astype(BF16)


def f32(x):
    return np.asarray(x, np.float32)


def f64(x):
    return np.asarray(x).astype(np.float64)


def striped(idx):
    return np.tile(idx.reshape(-1, 16).T, (8, 1))


V, E, F, HD, N = 4096, 128, 256, 128, 4096


def setup_inputs():
    return {"table": bf(np.random.standard_normal((E, V))), "w": bf(np.random.standard_normal((E, F)) / np.sqrt(E)), "v_w": bf(np.random.standard_normal((F, HD)) / np.sqrt(F)), "offs": striped(np.random.permutation(np.tile(np.arange(V), 2))[:N])}


def reference(table, w, v_w, offs):
    idx = offs[:16].T.reshape(-1)
    hf = np.maximum(f64(w).T @ f64(table)[:, idx], 0.0)
    return f64(v_w).T @ hf

@@ -1,0 +1,65 @@
+import concourse.mybir as mybir
+
+BF16, F32, U16 = mybir.dt.bfloat16, mybir.dt.float32, mybir.dt.uint16
+RELU = mybir.ActivationFunctionType.Relu
+
+P = 128
+V = 4096
+F = 256
+HD = 128
+N = 4096
+F_BLOCKS = F // P
+PIECE = 512
+PIECES = N // PIECE
+PIECE_OFFS = PIECE // 16
+
+FLOPS = 2 * P * F * N + 2 * F * HD * N
+
+
+def tile_modelconcept2_kernel(tc, table, w, v_w, offs, out):
+    nc = tc.nc
+    with (
+        tc.tile_pool(name="held", bufs=1) as held,
+        tc.tile_pool(name="values_pool", bufs=4) as values_pool,
+        tc.psum_pool(name="psum", bufs=8) as psum,
+    ):
+        offsets = held.tile([P, N // 16], U16, name="offsets")
+        nc.sync.dma_start(offsets[:], offs)
+        table_sb = held.tile([P, V], BF16, name="table_sb")
+        nc.sync.dma_start(table_sb[:], table)
+        w_sb = held.tile([P, F], BF16, name="w_sb")
+        nc.scalar.dma_start(w_sb[:], w)
+        vw_sb = held.tile([P, F_BLOCKS * HD], BF16, name="vw_sb")
+        for b in range(F_BLOCKS):
+            nc.scalar.dma_start(vw_sb[:, b * HD : (b + 1) * HD], v_w[b * P : (b + 1) * P, :])
+
+        hidden_sb = held.tile([P, F_BLOCKS * N], BF16, name="hidden_sb")
+
+
+        for piece in range(PIECES):
+            looked_up = table_sb[:].indirect(offsets[:, piece * PIECE_OFFS : (piece + 1) * PIECE_OFFS])
+            for b in range(F_BLOCKS):
+                hidden_ps = psum.tile([P, PIECE], F32, tag="bank")
+                nc.tensor.matmul(hidden_ps[:], w_sb[:, b * P : (b + 1) * P], looked_up, start=True, stop=True)
+                hidden_piece = hidden_sb[:, b * N + piece * PIECE : b * N + (piece + 1) * PIECE]
+                if b == 0:
+                    nc.scalar.activation(hidden_piece, hidden_ps[:], RELU)
+                else:
+                    nc.vector.tensor_scalar_max(hidden_piece, hidden_ps[:], 0.0)
+
+        for piece in range(PIECES):
+            values_ps = psum.tile([P, PIECE], F32, tag="bank")
+            for b in range(F_BLOCKS):
+                nc.tensor.matmul(
+                    values_ps[:],
+                    vw_sb[:, b * HD : (b + 1) * HD],
+                    hidden_sb[:, b * N + piece * PIECE : b * N + (piece + 1) * PIECE],
+                    start=(b == 0),
+                    stop=(b == F_BLOCKS - 1),
+                )
+            values_sb = values_pool.tile([P, PIECE], F32, name="values_sb")
+            if piece % 2 == 0:
+                nc.scalar.copy(values_sb[:], values_ps[:])
+            else:
+                nc.vector.tensor_copy(values_sb[:], values_ps[:])
+            nc.sync.dma_start(out[:, piece * PIECE : (piece + 1) * PIECE], values_sb[:])

@@ -20,7 +20,6 @@ def tile_modelconcept2_kernel(tc, table, w, v_w, offs, out):
     nc = tc.nc
     with (
         tc.tile_pool(name="held", bufs=1) as held,
-        tc.tile_pool(name="values_pool", bufs=4) as values_pool,
         tc.psum_pool(name="psum", bufs=8) as psum,
     ):
         offsets = held.tile([P, N // 16], U16, name="offsets")
@@ -34,6 +33,7 @@ def tile_modelconcept2_kernel(tc, table, w, v_w, offs, out):
             nc.scalar.dma_start(vw_sb[:, b * HD : (b + 1) * HD], v_w[b * P : (b + 1) * P, :])
 
         hidden_sb = held.tile([P, F_BLOCKS * N], BF16, name="hidden_sb")
+        values_sb = held.tile([P, N], F32, name="values_sb")
 
 
         for piece in range(PIECES):
@@ -57,9 +57,9 @@ def tile_modelconcept2_kernel(tc, table, w, v_w, offs, out):
                     start=(b == 0),
                     stop=(b == F_BLOCKS - 1),
                 )
-            values_sb = values_pool.tile([P, PIECE], F32, name="values_sb")
+            values_piece = values_sb[:, piece * PIECE : (piece + 1) * PIECE]
             if piece % 2 == 0:
-                nc.scalar.copy(values_sb[:], values_ps[:])
+                nc.scalar.copy(values_piece, values_ps[:])
             else:
-                nc.vector.tensor_copy(values_sb[:], values_ps[:])
-            nc.sync.dma_start(out[:, piece * PIECE : (piece + 1) * PIECE], values_sb[:])
+                nc.vector.tensor_copy(values_piece, values_ps[:])
+            nc.sync.dma_start(out[:, piece * PIECE : (piece + 1) * PIECE], values_piece)

@@ -12,6 +12,7 @@ F_BLOCKS = F // P
 PIECE = 512
 PIECES = N // PIECE
 PIECE_OFFS = PIECE // 16
+WARM_UP = 8
 
 FLOPS = 2 * P * F * N + 2 * F * HD * N
 
@@ -35,6 +36,12 @@ def tile_modelconcept2_kernel(tc, table, w, v_w, offs, out):
         hidden_sb = held.tile([P, F_BLOCKS * N], BF16, name="hidden_sb")
         values_sb = held.tile([P, N], F32, name="values_sb")
 
+
+        zeros = held.tile([P, PIECE], BF16, name="zeros")
+        nc.vector.memset(zeros[:], 0.0)
+        unread_ps = psum.tile([P, PIECE], F32, tag="bank")
+        for _ in range(WARM_UP):
+            nc.tensor.matmul(unread_ps[:], zeros[:, :P], zeros[:], start=True, stop=True)
 
         for piece in range(PIECES):
             looked_up = table_sb[:].indirect(offsets[:, piece * PIECE_OFFS : (piece + 1) * PIECE_OFFS])

@@ -12,7 +12,8 @@ F_BLOCKS = F // P
 PIECE = 512
 PIECES = N // PIECE
 PIECE_OFFS = PIECE // 16
-WARM_UP = 8
+HALF = PIECE // 2
+EARLY_PIECES = 6
 
 FLOPS = 2 * P * F * N + 2 * F * HD * N
 
@@ -37,13 +38,7 @@ def tile_modelconcept2_kernel(tc, table, w, v_w, offs, out):
         values_sb = held.tile([P, N], F32, name="values_sb")
 
 
-        zeros = held.tile([P, PIECE], BF16, name="zeros")
-        nc.vector.memset(zeros[:], 0.0)
-        unread_ps = psum.tile([P, PIECE], F32, tag="bank")
-        for _ in range(WARM_UP):
-            nc.tensor.matmul(unread_ps[:], zeros[:, :P], zeros[:], start=True, stop=True)
-
-        for piece in range(PIECES):
+        def first_layer(piece):
             looked_up = table_sb[:].indirect(offsets[:, piece * PIECE_OFFS : (piece + 1) * PIECE_OFFS])
             for b in range(F_BLOCKS):
                 hidden_ps = psum.tile([P, PIECE], F32, tag="bank")
@@ -54,19 +49,30 @@ def tile_modelconcept2_kernel(tc, table, w, v_w, offs, out):
                 else:
                     nc.vector.tensor_scalar_max(hidden_piece, hidden_ps[:], 0.0)
 
-        for piece in range(PIECES):
-            values_ps = psum.tile([P, PIECE], F32, tag="bank")
-            for b in range(F_BLOCKS):
-                nc.tensor.matmul(
-                    values_ps[:],
-                    vw_sb[:, b * HD : (b + 1) * HD],
-                    hidden_sb[:, b * N + piece * PIECE : b * N + (piece + 1) * PIECE],
-                    start=(b == 0),
-                    stop=(b == F_BLOCKS - 1),
-                )
-            values_piece = values_sb[:, piece * PIECE : (piece + 1) * PIECE]
-            if piece % 2 == 0:
-                nc.scalar.copy(values_piece, values_ps[:])
-            else:
-                nc.vector.tensor_copy(values_piece, values_ps[:])
-            nc.sync.dma_start(out[:, piece * PIECE : (piece + 1) * PIECE], values_piece)
+        def second_layer(piece):
+            for first in (piece * PIECE, piece * PIECE + HALF):
+                values_ps = psum.tile([P, HALF], F32, tag="bank")
+                for b in range(F_BLOCKS):
+                    nc.tensor.matmul(
+                        values_ps[:],
+                        vw_sb[:, b * HD : (b + 1) * HD],
+                        hidden_sb[:, b * N + first : b * N + first + HALF],
+                        start=(b == 0),
+                        stop=(b == F_BLOCKS - 1),
+                    )
+                if first == piece * PIECE:
+                    nc.scalar.copy(values_sb[:, first : first + HALF], values_ps[:])
+                else:
+                    nc.vector.tensor_copy(values_sb[:, first : first + HALF], values_ps[:])
+            nc.sync.dma_start(
+                out[:, piece * PIECE : (piece + 1) * PIECE], values_sb[:, piece * PIECE : (piece + 1) * PIECE]
+            )
+
+        for piece in range(EARLY_PIECES):
+            first_layer(piece)
+        for piece in range(EARLY_PIECES):
+            second_layer(piece)
+        for piece in range(EARLY_PIECES, PIECES):
+            first_layer(piece)
+        for piece in range(EARLY_PIECES, PIECES):
+            second_layer(piece)

@@ -27,12 +27,13 @@ def tile_modelconcept2_kernel(tc, table, w, v_w, offs, out):
         offsets = held.tile([P, N // 16], U16, name="offsets")
         nc.sync.dma_start(offsets[:], offs)
         table_sb = held.tile([P, V], BF16, name="table_sb")
-        nc.sync.dma_start(table_sb[:], table)
+        nc.sync.dma_start(table_sb[:, : V // 2], table[:, : V // 2])
+        nc.scalar.dma_start(table_sb[:, V // 2 :], table[:, V // 2 :])
         w_sb = held.tile([P, F], BF16, name="w_sb")
         nc.scalar.dma_start(w_sb[:], w)
         vw_sb = held.tile([P, F_BLOCKS * HD], BF16, name="vw_sb")
         for b in range(F_BLOCKS):
-            nc.scalar.dma_start(vw_sb[:, b * HD : (b + 1) * HD], v_w[b * P : (b + 1) * P, :])
+            nc.sync.dma_start(vw_sb[:, b * HD : (b + 1) * HD], v_w[b * P : (b + 1) * P, :])
 
         hidden_sb = held.tile([P, F_BLOCKS * N], BF16, name="hidden_sb")
         values_sb = held.tile([P, N], F32, name="values_sb")

@@ -11,7 +11,6 @@ N = 4096
 F_BLOCKS = F // P
 PIECE = 512
 PIECES = N // PIECE
-PIECE_OFFS = PIECE // 16
 HALF = PIECE // 2
 EARLY_PIECES = 6
 
@@ -39,18 +38,18 @@ def tile_modelconcept2_kernel(tc, table, w, v_w, offs, out):
         values_sb = held.tile([P, N], F32, name="values_sb")
 
 
-        def first_layer(piece):
-            looked_up = table_sb[:].indirect(offsets[:, piece * PIECE_OFFS : (piece + 1) * PIECE_OFFS])
+        def first_layer(first, width):
+            looked_up = table_sb[:].indirect(offsets[:, first // 16 : (first + width) // 16])
             for b in range(F_BLOCKS):
-                hidden_ps = psum.tile([P, PIECE], F32, tag="bank")
+                hidden_ps = psum.tile([P, width], F32, tag="bank")
                 nc.tensor.matmul(hidden_ps[:], w_sb[:, b * P : (b + 1) * P], looked_up, start=True, stop=True)
-                hidden_piece = hidden_sb[:, b * N + piece * PIECE : b * N + (piece + 1) * PIECE]
+                hidden_piece = hidden_sb[:, b * N + first : b * N + first + width]
                 if b == 0:
                     nc.scalar.activation(hidden_piece, hidden_ps[:], RELU)
                 else:
                     nc.vector.tensor_scalar_max(hidden_piece, hidden_ps[:], 0.0)
 
-        def second_layer(piece):
+        def second_layer(piece, stores):
             for first in (piece * PIECE, piece * PIECE + HALF):
                 values_ps = psum.tile([P, HALF], F32, tag="bank")
                 for b in range(F_BLOCKS):
@@ -65,15 +64,20 @@ def tile_modelconcept2_kernel(tc, table, w, v_w, offs, out):
                     nc.scalar.copy(values_sb[:, first : first + HALF], values_ps[:])
                 else:
                     nc.vector.tensor_copy(values_sb[:, first : first + HALF], values_ps[:])
-            nc.sync.dma_start(
-                out[:, piece * PIECE : (piece + 1) * PIECE], values_sb[:, piece * PIECE : (piece + 1) * PIECE]
-            )
+                if stores == 2:
+                    nc.sync.dma_start(out[:, first : first + HALF], values_sb[:, first : first + HALF])
+            if stores == 1:
+                nc.sync.dma_start(
+                    out[:, piece * PIECE : (piece + 1) * PIECE], values_sb[:, piece * PIECE : (piece + 1) * PIECE]
+                )
 
         for piece in range(EARLY_PIECES):
-            first_layer(piece)
+            first_layer(piece * PIECE, PIECE)
         for piece in range(EARLY_PIECES):
-            second_layer(piece)
+            second_layer(piece, stores=1)
+        for piece in range(EARLY_PIECES, PIECES - 1):
+            first_layer(piece * PIECE, PIECE)
+        for first in ((PIECES - 1) * PIECE, (PIECES - 1) * PIECE + HALF):
+            first_layer(first, HALF)
         for piece in range(EARLY_PIECES, PIECES):
-            first_layer(piece)
-        for piece in range(EARLY_PIECES, PIECES):
-            second_layer(piece)
+            second_layer(piece, stores=2 if piece == PIECES - 1 else 1)

@@ -12,7 +12,8 @@ F_BLOCKS = F // P
 PIECE = 512
 PIECES = N // PIECE
 HALF = PIECE // 2
-EARLY_PIECES = 6
+HALVES = N // HALF
+EARLY_HALVES = HALVES - 3
 
 FLOPS = 2 * P * F * N + 2 * F * HD * N
 
@@ -49,35 +50,34 @@ def tile_modelconcept2_kernel(tc, table, w, v_w, offs, out):
                 else:
                     nc.vector.tensor_scalar_max(hidden_piece, hidden_ps[:], 0.0)
 
-        def second_layer(piece, stores):
-            for first in (piece * PIECE, piece * PIECE + HALF):
-                values_ps = psum.tile([P, HALF], F32, tag="bank")
-                for b in range(F_BLOCKS):
-                    nc.tensor.matmul(
-                        values_ps[:],
-                        vw_sb[:, b * HD : (b + 1) * HD],
-                        hidden_sb[:, b * N + first : b * N + first + HALF],
-                        start=(b == 0),
-                        stop=(b == F_BLOCKS - 1),
-                    )
-                if first == piece * PIECE:
-                    nc.scalar.copy(values_sb[:, first : first + HALF], values_ps[:])
-                else:
-                    nc.vector.tensor_copy(values_sb[:, first : first + HALF], values_ps[:])
-                if stores == 2:
-                    nc.sync.dma_start(out[:, first : first + HALF], values_sb[:, first : first + HALF])
-            if stores == 1:
-                nc.sync.dma_start(
-                    out[:, piece * PIECE : (piece + 1) * PIECE], values_sb[:, piece * PIECE : (piece + 1) * PIECE]
+        def second_layer(half):
+            first = half * HALF
+            values_ps = psum.tile([P, HALF], F32, tag="bank")
+            for b in range(F_BLOCKS):
+                nc.tensor.matmul(
+                    values_ps[:],
+                    vw_sb[:, b * HD : (b + 1) * HD],
+                    hidden_sb[:, b * N + first : b * N + first + HALF],
+                    start=(b == 0),
+                    stop=(b == F_BLOCKS - 1),
                 )
+            if half % 2 == 0:
+                nc.scalar.copy(values_sb[:, first : first + HALF], values_ps[:])
+            else:
+                nc.vector.tensor_copy(values_sb[:, first : first + HALF], values_ps[:])
 
-        for piece in range(EARLY_PIECES):
+        def store(first, width):
+            nc.sync.dma_start(out[:, first : first + width], values_sb[:, first : first + width])
+
+        for piece in range(PIECES - 1):
             first_layer(piece * PIECE, PIECE)
-        for piece in range(EARLY_PIECES):
-            second_layer(piece, stores=1)
-        for piece in range(EARLY_PIECES, PIECES - 1):
-            first_layer(piece * PIECE, PIECE)
-        for first in ((PIECES - 1) * PIECE, (PIECES - 1) * PIECE + HALF):
-            first_layer(first, HALF)
-        for piece in range(EARLY_PIECES, PIECES):
-            second_layer(piece, stores=2 if piece == PIECES - 1 else 1)
+        for half in range(EARLY_HALVES):
+            second_layer(half)
+            if half % 2 == 1:
+                store((half - 1) * HALF, PIECE)
+        store((EARLY_HALVES - 1) * HALF, HALF)
+        for half in (HALVES - 2, HALVES - 1):
+            first_layer(half * HALF, HALF)
+        for half in range(EARLY_HALVES, HALVES):
+            second_layer(half)
+            store(half * HALF, HALF)

@@ -13,7 +13,7 @@ PIECE = 512
 PIECES = N // PIECE
 HALF = PIECE // 2
 HALVES = N // HALF
-EARLY_HALVES = HALVES - 3
+EARLY_HALVES = HALVES - 4
 
 FLOPS = 2 * P * F * N + 2 * F * HD * N
 
@@ -75,7 +75,6 @@ def tile_modelconcept2_kernel(tc, table, w, v_w, offs, out):
             second_layer(half)
             if half % 2 == 1:
                 store((half - 1) * HALF, PIECE)
-        store((EARLY_HALVES - 1) * HALF, HALF)
         for half in (HALVES - 2, HALVES - 1):
             first_layer(half * HALF, HALF)
         for half in range(EARLY_HALVES, HALVES):

@@ -33,7 +33,7 @@ def tile_modelconcept2_kernel(tc, table, w, v_w, offs, out):
         nc.scalar.dma_start(w_sb[:], w)
         vw_sb = held.tile([P, F_BLOCKS * HD], BF16, name="vw_sb")
         for b in range(F_BLOCKS):
-            nc.sync.dma_start(vw_sb[:, b * HD : (b + 1) * HD], v_w[b * P : (b + 1) * P, :])
+            nc.scalar.dma_start(vw_sb[:, b * HD : (b + 1) * HD], v_w[b * P : (b + 1) * P, :])
 
         hidden_sb = held.tile([P, F_BLOCKS * N], BF16, name="hidden_sb")
         values_sb = held.tile([P, N], F32, name="values_sb")

@@ -13,6 +13,7 @@ PIECE = 512
 PIECES = N // PIECE
 HALF = PIECE // 2
 HALVES = N // HALF
+QUARTER = PIECE // 4
 EARLY_HALVES = HALVES - 4
 
 FLOPS = 2 * P * F * N + 2 * F * HD * N
@@ -50,21 +51,20 @@ def tile_modelconcept2_kernel(tc, table, w, v_w, offs, out):
                 else:
                     nc.vector.tensor_scalar_max(hidden_piece, hidden_ps[:], 0.0)
 
-        def second_layer(half):
-            first = half * HALF
-            values_ps = psum.tile([P, HALF], F32, tag="bank")
+        def second_layer(first, width, through_scalar):
+            values_ps = psum.tile([P, width], F32, tag="bank")
             for b in range(F_BLOCKS):
                 nc.tensor.matmul(
                     values_ps[:],
                     vw_sb[:, b * HD : (b + 1) * HD],
-                    hidden_sb[:, b * N + first : b * N + first + HALF],
+                    hidden_sb[:, b * N + first : b * N + first + width],
                     start=(b == 0),
                     stop=(b == F_BLOCKS - 1),
                 )
-            if half % 2 == 0:
-                nc.scalar.copy(values_sb[:, first : first + HALF], values_ps[:])
+            if through_scalar:
+                nc.scalar.copy(values_sb[:, first : first + width], values_ps[:])
             else:
-                nc.vector.tensor_copy(values_sb[:, first : first + HALF], values_ps[:])
+                nc.vector.tensor_copy(values_sb[:, first : first + width], values_ps[:])
 
         def store(first, width):
             nc.sync.dma_start(out[:, first : first + width], values_sb[:, first : first + width])
@@ -72,11 +72,14 @@ def tile_modelconcept2_kernel(tc, table, w, v_w, offs, out):
         for piece in range(PIECES - 1):
             first_layer(piece * PIECE, PIECE)
         for half in range(EARLY_HALVES):
-            second_layer(half)
+            second_layer(half * HALF, HALF, half % 2 == 0)
             if half % 2 == 1:
                 store((half - 1) * HALF, PIECE)
         for half in (HALVES - 2, HALVES - 1):
             first_layer(half * HALF, HALF)
-        for half in range(EARLY_HALVES, HALVES):
-            second_layer(half)
+        for half in range(EARLY_HALVES, HALVES - 1):
+            second_layer(half * HALF, HALF, half % 2 == 0)
             store(half * HALF, HALF)
+        second_layer(N - HALF, QUARTER, False)
+        second_layer(N - QUARTER, QUARTER, True)
+        store(N - HALF, HALF)

@@ -73,7 +73,11 @@ def tile_modelconcept2_kernel(tc, table, w, v_w, offs, out):
             first_layer(piece * PIECE, PIECE)
         for half in range(EARLY_HALVES):
             second_layer(half * HALF, HALF, half % 2 == 0)
-            if half % 2 == 1:
+            if half < 2:
+                store(half * HALF, HALF)
+            elif half == EARLY_HALVES - 1:
+                store((half - 3) * HALF, 2 * PIECE)
+            elif half % 2 == 1 and half < EARLY_HALVES - 4:
                 store((half - 1) * HALF, PIECE)
         for half in (HALVES - 2, HALVES - 1):
             first_layer(half * HALF, HALF)

import concourse.mybir as mybir

BF16, F32, U16 = mybir.dt.bfloat16, mybir.dt.float32, mybir.dt.uint16
RELU = mybir.ActivationFunctionType.Relu

P = 128
V = 4096
F = 256
HD = 128
N = 4096
F_BLOCKS = F // P
PIECE = 512
PIECES = N // PIECE
HALF = PIECE // 2
HALVES = N // HALF
QUARTER = PIECE // 4
EARLY_HALVES = HALVES - 4

FLOPS = 2 * P * F * N + 2 * F * HD * N


def tile_modelconcept2_kernel(tc, table, w, v_w, offs, out):
    nc = tc.nc
    with (
        tc.tile_pool(name="held", bufs=1) as held,
        tc.psum_pool(name="psum", bufs=8) as psum,
    ):
        offsets = held.tile([P, N // 16], U16, name="offsets")
        nc.sync.dma_start(offsets[:], offs)
        table_sb = held.tile([P, V], BF16, name="table_sb")
        nc.sync.dma_start(table_sb[:, : V // 2], table[:, : V // 2])
        nc.scalar.dma_start(table_sb[:, V // 2 :], table[:, V // 2 :])
        w_sb = held.tile([P, F], BF16, name="w_sb")
        nc.scalar.dma_start(w_sb[:], w)
        vw_sb = held.tile([P, F_BLOCKS * HD], BF16, name="vw_sb")
        for b in range(F_BLOCKS):
            nc.scalar.dma_start(vw_sb[:, b * HD : (b + 1) * HD], v_w[b * P : (b + 1) * P, :])

        hidden_sb = held.tile([P, F_BLOCKS * N], BF16, name="hidden_sb")
        values_sb = held.tile([P, N], F32, name="values_sb")


        def first_layer(first, width):
            looked_up = table_sb[:].indirect(offsets[:, first // 16 : (first + width) // 16])
            for b in range(F_BLOCKS):
                hidden_ps = psum.tile([P, width], F32, tag="bank")
                nc.tensor.matmul(hidden_ps[:], w_sb[:, b * P : (b + 1) * P], looked_up, start=True, stop=True)
                hidden_piece = hidden_sb[:, b * N + first : b * N + first + width]
                if b == 0:
                    nc.scalar.activation(hidden_piece, hidden_ps[:], RELU)
                else:
                    nc.vector.tensor_scalar_max(hidden_piece, hidden_ps[:], 0.0)

        def second_layer(first, width, through_scalar):
            values_ps = psum.tile([P, width], F32, tag="bank")
            for b in range(F_BLOCKS):
                nc.tensor.matmul(
                    values_ps[:],
                    vw_sb[:, b * HD : (b + 1) * HD],
                    hidden_sb[:, b * N + first : b * N + first + width],
                    start=(b == 0),
                    stop=(b == F_BLOCKS - 1),
                )
            if through_scalar:
                nc.scalar.copy(values_sb[:, first : first + width], values_ps[:])
            else:
                nc.vector.tensor_copy(values_sb[:, first : first + width], values_ps[:])

        def store(first, width):
            nc.sync.dma_start(out[:, first : first + width], values_sb[:, first : first + width])

        for piece in range(PIECES - 1):
            first_layer(piece * PIECE, PIECE)
        for half in range(EARLY_HALVES):
            second_layer(half * HALF, HALF, half % 2 == 0)
            if half < 2:
                store(half * HALF, HALF)
            elif half == EARLY_HALVES - 1:
                store((half - 3) * HALF, 2 * PIECE)
            elif half % 2 == 1 and half < EARLY_HALVES - 4:
                store((half - 1) * HALF, PIECE)
        for half in (HALVES - 2, HALVES - 1):
            first_layer(half * HALF, HALF)
        for half in range(EARLY_HALVES, HALVES - 1):
            second_layer(half * HALF, HALF, half % 2 == 0)
            store(half * HALF, HALF)
        second_layer(N - HALF, QUARTER, False)
        second_layer(N - QUARTER, QUARTER, True)
        store(N - HALF, HALF)
